import numpy as np
import ml_dtypes


def mxq(x, axis, fmt="e4m3"):
    dtype, down = {"e4m3": (ml_dtypes.float8_e4m3fn, 7), "e5m2": (ml_dtypes.float8_e5m2, 14)}[fmt]
    v = np.moveaxis(np.asarray(x, np.float32).astype(ml_dtypes.bfloat16).astype(np.float64), axis, -1)
    blocks = v.reshape(v.shape[:-1] + (-1, 32))
    amax = np.abs(blocks).max(-1, keepdims=True)
    byte = np.maximum(np.where(amax > 0, np.frexp(amax)[1] - 1 + 127, 0) - down, 1)
    scale = np.exp2(byte - 127.0)
    codes = (blocks / scale).astype(np.float32).astype(dtype).astype(np.float64)
    return np.moveaxis((codes * scale).reshape(v.shape), -1, axis)


WIDE = False


def mx_kscale(k):
    if not WIDE:
        return np.ones(k)
    levels = np.array([10, -10, 5, -5, 0])
    a = np.random.permutation(np.resize(levels, k // 512 * 4)).reshape(k // 512, 4)
    idx = np.arange(k)
    return np.exp2(a[idx // 512, idx % 128 // 32])


BF16 = ml_dtypes.bfloat16


def bf(x):
    return np.asarray(x, np.float32).astype(BF16)


def f64(x):
    return np.asarray(x).astype(np.float64)


E2M1 = np.array([0.0, 0.5, 1.0, 1.5, 2.0, 3.0, 4.0, 6.0, -0.0, -0.5, -1.0, -1.5, -2.0, -3.0, -4.0, -6.0])


def pack_weight(w, fmt):
    k, n = w.shape
    w = f64(bf(w)).reshape(k // 32, 32, n)
    amax = np.abs(w).max(1)
    if fmt == "e4m3":
        byte = np.frexp(amax)[1] - 1 + 127 - 7
    else:
        mant, ex = np.frexp(amax / 6.0)
        byte = np.where(mant > 0.5, ex, ex - 1) + 127
    byte = np.clip(np.where(amax > 0, byte, 1), 1, 254)
    scaled = (w * np.exp2(127.0 - byte)[:, None, :]).reshape(k, n).astype(np.float32)
    by_word = np.ascontiguousarray(scaled.reshape(k // 512, 128, 4, n).transpose(0, 1, 3, 2))
    if fmt == "e4m3":
        words = by_word.astype(ml_dtypes.float8_e4m3fn).view(np.uint8)
    else:
        c = by_word.astype(ml_dtypes.float4_e2m1fn).view(np.uint8) & 0xF
        words = c[..., 0::2] | (c[..., 1::2] << 4)
    return np.ascontiguousarray(words), np.ascontiguousarray(byte.astype(np.uint8).reshape(k // 512, 16, n))


def unpack_weight(words, scales, fmt):
    g, p, n, _ = words.shape
    if fmt == "e4m3":
        vals = np.ascontiguousarray(words).view(ml_dtypes.float8_e4m3fn).astype(np.float64)
    else:
        nib = np.empty((g, p, n, 4), np.uint8)
        nib[..., 0::2] = words & 0xF
        nib[..., 1::2] = words >> 4
        vals = E2M1[nib]
    vals = vals * np.repeat(np.exp2(scales.astype(np.float64) - 127.0), 8, axis=1)[..., None]
    return vals.transpose(0, 1, 3, 2).reshape(g * 512, n)

def pack4(w):
    words, scales = pack_weight(w, "e2m1")
    return words.reshape(words.shape[0], 128, -1), scales


def unpack4(words, scales):
    return unpack_weight(words.reshape(words.shape[0], 128, -1, 2), scales, "e2m1")


M, K = 512, 3072
N_Q, N_K, N_V = 1024, 1024, 1024
N = N_Q + N_K + N_V


def setup_inputs():
    s = mx_kscale(K)
    x = bf(np.random.standard_normal((M, K)) * s)
    words, scales = pack4(np.random.standard_normal((K, N)) * 0.018 / s[:, None])
    w_scale = bf(0.5 + np.random.random((1, N)))
    bias = bf(np.random.standard_normal(N) * 0.3)
    return {"x": x,
            "weight_fp8_t_words": words,
            "weight_fp8_t_scales": scales,
            "w_scale": w_scale,
            "bias": bias}


def reference(x, weight_fp8_t_words, weight_fp8_t_scales, w_scale, bias):
    acc = mxq(f64(x), 1, "e4m3") @ unpack4(weight_fp8_t_words, weight_fp8_t_scales)
    out = acc * f64(w_scale) + f64(bias)
    q = out[:, :N_Q]
    k = out[:, N_Q:N_Q + N_K]
    v = out[:, N_Q + N_K:]
    return (q, k, v)

@@ -1,0 +1,165 @@
+from contextlib import ExitStack
+
+import concourse.mybir as mybir
+from concourse.masks import make_identity
+
+F32 = mybir.dt.float32
+BF16 = mybir.dt.bfloat16
+I32 = mybir.dt.int32
+U32 = mybir.dt.uint32
+U8 = mybir.dt.uint8
+FP8X4 = mybir.dt.float8_e4m3fn_x4
+FP4X4 = mybir.dt.float4_e2m1fn_x4
+MULT = mybir.AluOpType.mult
+ADD = mybir.AluOpType.add
+
+P = 128
+M, K, N = 512, 3072, 3072
+K_PASS = 512
+G = K // K_PASS
+MT = M // P
+NB = 512
+N_OUT = 1024
+FLOPS = 2 * M * K * N
+
+
+def tile_fusedqkvfp8linear_kernel(
+    tc, x, weight_fp8_t_words, weight_fp8_t_scales, w_scale, bias, out_0, out_1, out_2
+):
+    nc = tc.nc
+    outs = (out_0, out_1, out_2)
+    words_i32 = weight_fp8_t_words.bitcast(I32).rearrange("g p b -> p g b")
+    scales_i32 = weight_fp8_t_scales.bitcast(I32).rearrange("g (q r) n -> r q g n", r=4)
+
+    with ExitStack() as ctx:
+        ctx.enter_context(tc.manual_schedule())
+        keep = ctx.enter_context(tc.tile_pool(name="keep", bufs=1))
+        stage = ctx.enter_context(tc.tile_pool(name="stage", bufs=4))
+        results = ctx.enter_context(tc.tile_pool(name="results", bufs=6))
+        ps_small = ctx.enter_context(tc.psum_pool(name="ps_small", bufs=3))
+        ps_acc = ctx.enter_context(tc.psum_pool(name="ps_acc", bufs=5))
+
+        x_sb = [keep.tile([P, K], BF16, name="x_sb%d" % mt) for mt in range(MT)]
+        w_sb = keep.tile([P, G, 2 * N], U8, align_bytes=64)
+        w_planes = keep.tile([P, G, N], U8, align_bytes=64)
+        x_codes = keep.tile([P, MT, G, P], U32, align_bytes=64)
+        x_planes = keep.tile([P, MT, G, P], U8, align_bytes=64)
+        ident_b = keep.tile([P, P], BF16)
+        ident_f = keep.tile([P, P], F32)
+        rows = keep.tile([P, NB], BF16)
+        spread = keep.tile([P, 2 * N], BF16)
+
+        nc.vector.memset(rows[:], 0.0)
+        nc.scalar.dma_start(out=rows[0:6, :], in_=w_scale.rearrange("o (r c) -> (o r) c", c=NB))
+        nc.scalar.dma_start(out=rows[6:12, :], in_=bias.rearrange("(r c) -> r c", c=NB))
+        make_identity(nc, ident_b[:])
+        make_identity(nc, ident_f[:])
+
+        def load_x(mt):
+            nc.sync.dma_start(out=x_sb[mt][:], in_=x[P * mt : P * (mt + 1), :])
+
+        def load_scales(n0, n1):
+            nc.vector.memset(w_planes[:, :, n0:n1].bitcast(I32), 0)
+            for r in range(4):
+                nc.sync.dma_start(
+                    out=w_planes[r:P:32, :, n0:n1].bitcast(I32),
+                    in_=scales_i32[r][:, :, n0 // 4 : n1 // 4],
+                )
+
+        def load_words(n0, n1):
+            nc.sync.dma_start(
+                out=w_sb[:, :, 2 * n0 : 2 * n1].bitcast(I32),
+                in_=words_i32[:, :, n0 // 2 : n1 // 2],
+            )
+
+        load_x(0)
+        load_x(1)
+        load_scales(0, N_OUT)
+        load_words(0, N_OUT)
+        load_x(2)
+        load_x(3)
+        load_scales(N_OUT, N)
+        load_words(N_OUT, 2 * N_OUT)
+        load_words(2 * N_OUT, N)
+
+        def spread_rows(r0):
+            bank = ps_small.tile([P, 2 * NB], BF16, tag="small")
+            for i in range(2):
+                nc.tensor.matmul(
+                    out=bank[:, NB * i : NB * (i + 1)],
+                    lhsT=ident_b[:, r0 + i : r0 + i + 1].to_broadcast([P, P]),
+                    rhs=rows[:],
+                    start=True,
+                    stop=True,
+                )
+            nc.scalar.copy(out=spread[:, NB * r0 : NB * (r0 + 2)], in_=bank[:])
+
+        def transpose_x(mt):
+            x_words = x_sb[mt][:].bitcast(F32)
+            grouped = []
+            for h in range(G // 2):
+                bank = ps_small.tile([P, 2, 2, P], F32, tag="small")
+                for gg in range(2):
+                    g = 2 * h + gg
+                    for u in range(2):
+                        nc.tensor.transpose(
+                            bank[:, gg, u, :], x_words[:, 256 * g + u : 256 * (g + 1) : 2], ident_f[:]
+                        )
+                gr = stage.tile([P, 2, P, 4], BF16, align_bytes=64, tag="grouped")
+                nc.scalar.copy(out=gr[:].bitcast(F32), in_=bank[:].rearrange("p g u m -> p g m u"))
+                grouped.append(gr)
+            return grouped
+
+        def quantise_x(mt, grouped):
+            for h in range(G // 2):
+                nc.vector.quantize_mx(
+                    out=x_codes[:, mt, 2 * h : 2 * h + 2, :].rearrange("p g m -> p (g m)").bitcast(FP8X4),
+                    scales=x_planes[:, mt, 2 * h : 2 * h + 2, :].rearrange("p g m -> p (g m)"),
+                    in_=grouped[h][:].rearrange("p g m t -> p (g m t)"),
+                )
+
+        def product(mt, jp):
+            res = results.tile([P, N_OUT], F32, tag="res")
+            last = mt == MT - 1 and jp == 2
+            for i in range(2):
+                j = 2 * jp + i
+                acc = ps_acc.tile([P, NB], F32, tag="acc")
+                for g in range(G):
+                    nc.tensor.matmul_mx(
+                        out=acc[:],
+                        lhsT=x_codes[:, mt, g, :].bitcast(FP8X4),
+                        lhsT_scale=x_planes[:, mt, g, :],
+                        rhs=w_sb[:, g, 2 * NB * j : 2 * NB * (j + 1)].bitcast(FP4X4),
+                        rhs_scale=w_planes[:, g, NB * j : NB * (j + 1)],
+                        start=(g == 0),
+                        stop=(g == G - 1),
+                    )
+                half = res[:, NB * i : NB * (i + 1)]
+                nc.vector.tensor_tensor(out=half, in0=acc[:], in1=spread[:, NB * j : NB * (j + 1)], op=MULT)
+                nc.vector.tensor_tensor(out=half, in0=half, in1=spread[:, N + NB * j : N + NB * (j + 1)], op=ADD)
+                if last:
+                    nc.sync.dma_start(out=outs[jp][P * mt : P * (mt + 1), NB * i : NB * (i + 1)], in_=half)
+            if not last:
+                nc.sync.dma_start(out=outs[jp][P * mt : P * (mt + 1), :], in_=res[:])
+
+        spread_rows(0)
+        spread_rows(6)
+        g0 = transpose_x(0)
+        spread_rows(2)
+        spread_rows(8)
+        quantise_x(0, g0)
+        g1 = transpose_x(1)
+        spread_rows(4)
+        spread_rows(10)
+        quantise_x(1, g1)
+        product(0, 0)
+        g2 = transpose_x(2)
+        quantise_x(2, g2)
+        product(1, 0)
+        g3 = transpose_x(3)
+        quantise_x(3, g3)
+        product(2, 0)
+        product(3, 0)
+        for jp in range(1, 3):
+            for mt in range(MT):
+                product(mt, jp)

@@ -23,6 +23,9 @@ N_OUT = 1024
 FLOPS = 2 * M * K * N
 
 
+CHUNKS = ((0, 1), (1, 2), (2, 4), (4, 6))
+
+
 def tile_fusedqkvfp8linear_kernel(
     tc, x, weight_fp8_t_words, weight_fp8_t_scales, w_scale, bias, out_0, out_1, out_2
 ):
@@ -35,13 +38,17 @@ def tile_fusedqkvfp8linear_kernel(
         ctx.enter_context(tc.manual_schedule())
         keep = ctx.enter_context(tc.tile_pool(name="keep", bufs=1))
         stage = ctx.enter_context(tc.tile_pool(name="stage", bufs=4))
-        results = ctx.enter_context(tc.tile_pool(name="results", bufs=6))
+        results = ctx.enter_context(tc.tile_pool(name="results", bufs=10))
         ps_small = ctx.enter_context(tc.psum_pool(name="ps_small", bufs=3))
         ps_acc = ctx.enter_context(tc.psum_pool(name="ps_acc", bufs=5))
 
         x_sb = [keep.tile([P, K], BF16, name="x_sb%d" % mt) for mt in range(MT)]
-        w_sb = keep.tile([P, G, 2 * N], U8, align_bytes=64)
-        w_planes = keep.tile([P, G, N], U8, align_bytes=64)
+        w_sb = [
+            keep.tile([P, G, 2 * NB * (j1 - j0)], U8, align_bytes=64, name="w_sb%d" % j0) for j0, j1 in CHUNKS
+        ]
+        w_planes = [
+            keep.tile([P, G, NB * (j1 - j0)], U8, align_bytes=64, name="w_planes%d" % j0) for j0, j1 in CHUNKS
+        ]
         x_codes = keep.tile([P, MT, G, P], U32, align_bytes=64)
         x_planes = keep.tile([P, MT, G, P], U8, align_bytes=64)
         ident_b = keep.tile([P, P], BF16)
@@ -49,38 +56,33 @@ def tile_fusedqkvfp8linear_kernel(
         rows = keep.tile([P, NB], BF16)
         spread = keep.tile([P, 2 * N], BF16)
 
-        nc.vector.memset(rows[:], 0.0)
-        nc.scalar.dma_start(out=rows[0:6, :], in_=w_scale.rearrange("o (r c) -> (o r) c", c=NB))
-        nc.scalar.dma_start(out=rows[6:12, :], in_=bias.rearrange("(r c) -> r c", c=NB))
+        nc.gpsimd.memset(rows[:], 0.0)
+        nc.sync.dma_start(out=rows[0:6, :], in_=w_scale.rearrange("o (r c) -> (o r) c", c=NB))
+        nc.sync.dma_start(out=rows[6:12, :], in_=bias.rearrange("(r c) -> r c", c=NB))
         make_identity(nc, ident_b[:])
         make_identity(nc, ident_f[:])
 
         def load_x(mt):
             nc.sync.dma_start(out=x_sb[mt][:], in_=x[P * mt : P * (mt + 1), :])
 
-        def load_scales(n0, n1):
-            nc.vector.memset(w_planes[:, :, n0:n1].bitcast(I32), 0)
+        def load_weight(c):
+            j0, j1 = CHUNKS[c]
+            nc.vector.memset(w_planes[c][:].bitcast(I32), 0)
             for r in range(4):
                 nc.sync.dma_start(
-                    out=w_planes[r:P:32, :, n0:n1].bitcast(I32),
-                    in_=scales_i32[r][:, :, n0 // 4 : n1 // 4],
+                    out=w_planes[c][r:P:32, :, :].bitcast(I32),
+                    in_=scales_i32[r][:, :, NB // 4 * j0 : NB // 4 * j1],
                 )
-
-        def load_words(n0, n1):
-            nc.sync.dma_start(
-                out=w_sb[:, :, 2 * n0 : 2 * n1].bitcast(I32),
-                in_=words_i32[:, :, n0 // 2 : n1 // 2],
-            )
+            nc.sync.dma_start(out=w_sb[c][:].bitcast(I32), in_=words_i32[:, :, NB // 2 * j0 : NB // 2 * j1])
 
         load_x(0)
+        load_weight(0)
         load_x(1)
-        load_scales(0, N_OUT)
-        load_words(0, N_OUT)
+        load_weight(1)
         load_x(2)
         load_x(3)
-        load_scales(N_OUT, N)
-        load_words(N_OUT, 2 * N_OUT)
-        load_words(2 * N_OUT, N)
+        load_weight(2)
+        load_weight(3)
 
         def spread_rows(r0):
             bank = ps_small.tile([P, 2 * NB], BF16, tag="small")
@@ -118,48 +120,48 @@ def tile_fusedqkvfp8linear_kernel(
                     in_=grouped[h][:].rearrange("p g m t -> p (g m t)"),
                 )
 
-        def product(mt, jp):
-            res = results.tile([P, N_OUT], F32, tag="res")
-            last = mt == MT - 1 and jp == 2
-            for i in range(2):
-                j = 2 * jp + i
-                acc = ps_acc.tile([P, NB], F32, tag="acc")
-                for g in range(G):
-                    nc.tensor.matmul_mx(
-                        out=acc[:],
-                        lhsT=x_codes[:, mt, g, :].bitcast(FP8X4),
-                        lhsT_scale=x_planes[:, mt, g, :],
-                        rhs=w_sb[:, g, 2 * NB * j : 2 * NB * (j + 1)].bitcast(FP4X4),
-                        rhs_scale=w_planes[:, g, NB * j : NB * (j + 1)],
-                        start=(g == 0),
-                        stop=(g == G - 1),
-                    )
-                half = res[:, NB * i : NB * (i + 1)]
-                nc.vector.tensor_tensor(out=half, in0=acc[:], in1=spread[:, NB * j : NB * (j + 1)], op=MULT)
-                nc.vector.tensor_tensor(out=half, in0=half, in1=spread[:, N + NB * j : N + NB * (j + 1)], op=ADD)
-                if last:
-                    nc.sync.dma_start(out=outs[jp][P * mt : P * (mt + 1), NB * i : NB * (i + 1)], in_=half)
-            if not last:
-                nc.sync.dma_start(out=outs[jp][P * mt : P * (mt + 1), :], in_=res[:])
+        def multiply(mt, j):
+            c = [i for i in range(len(CHUNKS)) if CHUNKS[i][0] <= j < CHUNKS[i][1]][0]
+            i = j - CHUNKS[c][0]
+            acc = ps_acc.tile([P, NB], F32, tag="acc")
+            for g in range(G):
+                nc.tensor.matmul_mx(
+                    out=acc[:],
+                    lhsT=x_codes[:, mt, g, :].bitcast(FP8X4),
+                    lhsT_scale=x_planes[:, mt, g, :],
+                    rhs=w_sb[c][:, g, 2 * NB * i : 2 * NB * (i + 1)].bitcast(FP4X4),
+                    rhs_scale=w_planes[c][:, g, NB * i : NB * (i + 1)],
+                    start=(g == 0),
+                    stop=(g == G - 1),
+                )
+            res = results.tile([P, NB], F32, tag="res")
+            nc.vector.tensor_tensor(out=res[:], in0=acc[:], in1=spread[:, NB * j : NB * (j + 1)], op=MULT)
+            return res
+
+        def finish(mt, j, res):
+            nc.vector.tensor_tensor(out=res[:], in0=res[:], in1=spread[:, N + NB * j : N + NB * (j + 1)], op=ADD)
+            nc.sync.dma_start(
+                out=outs[j // 2][P * mt : P * (mt + 1), NB * (j % 2) : NB * (j % 2 + 1)], in_=res[:]
+            )
+
+        jobs = [(0, 0), (1, 0), (0, 1), (1, 1), (2, 0), (2, 1), (3, 0), (3, 1)]
+        jobs.extend((mt, j) for jp in (1, 2) for mt in range(MT) for j in (2 * jp, 2 * jp + 1))
 
         spread_rows(0)
         spread_rows(6)
-        g0 = transpose_x(0)
+        grouped = transpose_x(0)
         spread_rows(2)
         spread_rows(8)
-        quantise_x(0, g0)
-        g1 = transpose_x(1)
-        spread_rows(4)
-        spread_rows(10)
-        quantise_x(1, g1)
-        product(0, 0)
-        g2 = transpose_x(2)
-        quantise_x(2, g2)
-        product(1, 0)
-        g3 = transpose_x(3)
-        quantise_x(3, g3)
-        product(2, 0)
-        product(3, 0)
-        for jp in range(1, 3):
-            for mt in range(MT):
-                product(mt, jp)
+        quantise_x(0, grouped)
+        waiting = None
+        for n, (mt, j) in enumerate(jobs):
+            if n == 1:
+                spread_rows(4)
+                spread_rows(10)
+            if n in (1, 4, 6):
+                quantise_x(mt, transpose_x(mt))
+            res = multiply(mt, j)
+            if waiting is not None:
+                finish(*waiting)
+            waiting = (mt, j, res)
+        finish(*waiting)

@@ -49,6 +49,7 @@ def tile_fusedqkvfp8linear_kernel(
         w_planes = [
             keep.tile([P, G, NB * (j1 - j0)], U8, align_bytes=64, name="w_planes%d" % j0) for j0, j1 in CHUNKS
         ]
+        x_sorted = [keep.tile([P, G, 2, P], F32, name="x_sorted%d" % mt) for mt in range(MT)]
         x_codes = keep.tile([P, MT, G, P], U32, align_bytes=64)
         x_planes = keep.tile([P, MT, G, P], U8, align_bytes=64)
         ident_b = keep.tile([P, P], BF16)
@@ -96,17 +97,22 @@ def tile_fusedqkvfp8linear_kernel(
                 )
             nc.scalar.copy(out=spread[:, NB * r0 : NB * (r0 + 2)], in_=bank[:])
 
+        def sort_x(mt, shared):
+            words = x_sb[mt][:].bitcast(F32).rearrange("p (g q u) -> p g u q", q=P, u=2)
+            if shared:
+                nc.vector.tensor_copy(out=x_sorted[mt][:, 0 : G // 2], in_=words[:, 0 : G // 2])
+                nc.scalar.copy(out=x_sorted[mt][:, G // 2 : G], in_=words[:, G // 2 : G])
+            else:
+                nc.scalar.copy(out=x_sorted[mt][:], in_=words)
+
         def transpose_x(mt):
-            x_words = x_sb[mt][:].bitcast(F32)
             grouped = []
             for h in range(G // 2):
                 bank = ps_small.tile([P, 2, 2, P], F32, tag="small")
                 for gg in range(2):
                     g = 2 * h + gg
                     for u in range(2):
-                        nc.tensor.transpose(
-                            bank[:, gg, u, :], x_words[:, 256 * g + u : 256 * (g + 1) : 2], ident_f[:]
-                        )
+                        nc.tensor.transpose(bank[:, gg, u, :], x_sorted[mt][:, g, u, :], ident_f[:])
                 gr = stage.tile([P, 2, P, 4], BF16, align_bytes=64, tag="grouped")
                 nc.scalar.copy(out=gr[:].bitcast(F32), in_=bank[:].rearrange("p g u m -> p g m u"))
                 grouped.append(gr)
@@ -147,17 +153,23 @@ def tile_fusedqkvfp8linear_kernel(
         jobs = [(0, 0), (1, 0), (0, 1), (1, 1), (2, 0), (2, 1), (3, 0), (3, 1)]
         jobs.extend((mt, j) for jp in (1, 2) for mt in range(MT) for j in (2 * jp, 2 * jp + 1))
 
+        sort_x(0, True)
         spread_rows(0)
         spread_rows(6)
         grouped = transpose_x(0)
         spread_rows(2)
         spread_rows(8)
         quantise_x(0, grouped)
+        sort_x(1, True)
         waiting = None
         for n, (mt, j) in enumerate(jobs):
             if n == 1:
                 spread_rows(4)
                 spread_rows(10)
+            if n == 2:
+                sort_x(2, False)
+            if n == 5:
+                sort_x(3, False)
             if n in (1, 4, 6):
                 quantise_x(mt, transpose_x(mt))
             res = multiply(mt, j)

@@ -32,7 +32,7 @@ def tile_fusedqkvfp8linear_kernel(
     nc = tc.nc
     outs = (out_0, out_1, out_2)
     words_i32 = weight_fp8_t_words.bitcast(I32).rearrange("g p b -> p g b")
-    scales_i32 = weight_fp8_t_scales.bitcast(I32).rearrange("g (q r) n -> r q g n", r=4)
+    scales_f32 = weight_fp8_t_scales.bitcast(F32).rearrange("g (q r) n -> r q g n", r=4)
 
     with ExitStack() as ctx:
         ctx.enter_context(tc.manual_schedule())
@@ -46,10 +46,7 @@ def tile_fusedqkvfp8linear_kernel(
         w_sb = [
             keep.tile([P, G, 2 * NB * (j1 - j0)], U8, align_bytes=64, name="w_sb%d" % j0) for j0, j1 in CHUNKS
         ]
-        w_planes = [
-            keep.tile([P, G, NB * (j1 - j0)], U8, align_bytes=64, name="w_planes%d" % j0) for j0, j1 in CHUNKS
-        ]
-        x_sorted = [keep.tile([P, G, 2, P], F32, name="x_sorted%d" % mt) for mt in range(MT)]
+        w_planes = [keep.tile([P, G, N_OUT], U8, align_bytes=64, name="w_planes%d" % jp) for jp in range(3)]
         x_codes = keep.tile([P, MT, G, P], U32, align_bytes=64)
         x_planes = keep.tile([P, MT, G, P], U8, align_bytes=64)
         ident_b = keep.tile([P, P], BF16)
@@ -61,19 +58,25 @@ def tile_fusedqkvfp8linear_kernel(
         nc.sync.dma_start(out=rows[0:6, :], in_=w_scale.rearrange("o (r c) -> (o r) c", c=NB))
         nc.sync.dma_start(out=rows[6:12, :], in_=bias.rearrange("(r c) -> r c", c=NB))
         make_identity(nc, ident_b[:])
+
+        def load_scales(jp):
+            nc.vector.memset(w_planes[jp][:].bitcast(I32), 0)
+            for r in range(4):
+                nc.gpsimd.dma_start(
+                    out=w_planes[jp][r:P:32, :, :].bitcast(F32),
+                    in_=scales_f32[r][:, :, N_OUT // 4 * jp : N_OUT // 4 * (jp + 1)],
+                )
+
+        load_scales(0)
         make_identity(nc, ident_f[:])
+        load_scales(1)
+        load_scales(2)
 
         def load_x(mt):
             nc.sync.dma_start(out=x_sb[mt][:], in_=x[P * mt : P * (mt + 1), :])
 
         def load_weight(c):
             j0, j1 = CHUNKS[c]
-            nc.vector.memset(w_planes[c][:].bitcast(I32), 0)
-            for r in range(4):
-                nc.sync.dma_start(
-                    out=w_planes[c][r:P:32, :, :].bitcast(I32),
-                    in_=scales_i32[r][:, :, NB // 4 * j0 : NB // 4 * j1],
-                )
             nc.sync.dma_start(out=w_sb[c][:].bitcast(I32), in_=words_i32[:, :, NB // 2 * j0 : NB // 2 * j1])
 
         load_x(0)
@@ -97,22 +100,17 @@ def tile_fusedqkvfp8linear_kernel(
                 )
             nc.scalar.copy(out=spread[:, NB * r0 : NB * (r0 + 2)], in_=bank[:])
 
-        def sort_x(mt, shared):
-            words = x_sb[mt][:].bitcast(F32).rearrange("p (g q u) -> p g u q", q=P, u=2)
-            if shared:
-                nc.vector.tensor_copy(out=x_sorted[mt][:, 0 : G // 2], in_=words[:, 0 : G // 2])
-                nc.scalar.copy(out=x_sorted[mt][:, G // 2 : G], in_=words[:, G // 2 : G])
-            else:
-                nc.scalar.copy(out=x_sorted[mt][:], in_=words)
-
         def transpose_x(mt):
+            x_words = x_sb[mt][:].bitcast(F32)
             grouped = []
             for h in range(G // 2):
                 bank = ps_small.tile([P, 2, 2, P], F32, tag="small")
                 for gg in range(2):
                     g = 2 * h + gg
                     for u in range(2):
-                        nc.tensor.transpose(bank[:, gg, u, :], x_sorted[mt][:, g, u, :], ident_f[:])
+                        nc.tensor.transpose(
+                            bank[:, gg, u, :], x_words[:, 256 * g + u : 256 * (g + 1) : 2], ident_f[:]
+                        )
                 gr = stage.tile([P, 2, P, 4], BF16, align_bytes=64, tag="grouped")
                 nc.scalar.copy(out=gr[:].bitcast(F32), in_=bank[:].rearrange("p g u m -> p g m u"))
                 grouped.append(gr)
@@ -136,7 +134,7 @@ def tile_fusedqkvfp8linear_kernel(
                     lhsT=x_codes[:, mt, g, :].bitcast(FP8X4),
                     lhsT_scale=x_planes[:, mt, g, :],
                     rhs=w_sb[c][:, g, 2 * NB * i : 2 * NB * (i + 1)].bitcast(FP4X4),
-                    rhs_scale=w_planes[c][:, g, NB * i : NB * (i + 1)],
+                    rhs_scale=w_planes[j // 2][:, g, NB * (j % 2) : NB * (j % 2 + 1)],
                     start=(g == 0),
                     stop=(g == G - 1),
                 )
@@ -153,23 +151,17 @@ def tile_fusedqkvfp8linear_kernel(
         jobs = [(0, 0), (1, 0), (0, 1), (1, 1), (2, 0), (2, 1), (3, 0), (3, 1)]
         jobs.extend((mt, j) for jp in (1, 2) for mt in range(MT) for j in (2 * jp, 2 * jp + 1))
 
-        sort_x(0, True)
         spread_rows(0)
         spread_rows(6)
         grouped = transpose_x(0)
         spread_rows(2)
         spread_rows(8)
         quantise_x(0, grouped)
-        sort_x(1, True)
         waiting = None
         for n, (mt, j) in enumerate(jobs):
             if n == 1:
                 spread_rows(4)
                 spread_rows(10)
-            if n == 2:
-                sort_x(2, False)
-            if n == 5:
-                sort_x(3, False)
             if n in (1, 4, 6):
                 quantise_x(mt, transpose_x(mt))
             res = multiply(mt, j)

@@ -32,13 +32,13 @@ def tile_fusedqkvfp8linear_kernel(
     nc = tc.nc
     outs = (out_0, out_1, out_2)
     words_i32 = weight_fp8_t_words.bitcast(I32).rearrange("g p b -> p g b")
-    scales_f32 = weight_fp8_t_scales.bitcast(F32).rearrange("g (q r) n -> r q g n", r=4)
+    scales_i32 = weight_fp8_t_scales.bitcast(I32).rearrange("g (q r) n -> r q g n", r=4)
 
     with ExitStack() as ctx:
         ctx.enter_context(tc.manual_schedule())
         keep = ctx.enter_context(tc.tile_pool(name="keep", bufs=1))
         stage = ctx.enter_context(tc.tile_pool(name="stage", bufs=4))
-        results = ctx.enter_context(tc.tile_pool(name="results", bufs=10))
+        results = ctx.enter_context(tc.tile_pool(name="results", bufs=8))
         ps_small = ctx.enter_context(tc.psum_pool(name="ps_small", bufs=3))
         ps_acc = ctx.enter_context(tc.psum_pool(name="ps_acc", bufs=5))
 
@@ -46,7 +46,9 @@ def tile_fusedqkvfp8linear_kernel(
         w_sb = [
             keep.tile([P, G, 2 * NB * (j1 - j0)], U8, align_bytes=64, name="w_sb%d" % j0) for j0, j1 in CHUNKS
         ]
-        w_planes = [keep.tile([P, G, N_OUT], U8, align_bytes=64, name="w_planes%d" % jp) for jp in range(3)]
+        w_planes = [
+            keep.tile([P, G, NB * (j1 - j0)], U8, align_bytes=64, name="w_planes%d" % j0) for j0, j1 in CHUNKS
+        ]
         x_codes = keep.tile([P, MT, G, P], U32, align_bytes=64)
         x_planes = keep.tile([P, MT, G, P], U8, align_bytes=64)
         ident_b = keep.tile([P, P], BF16)
@@ -58,25 +60,19 @@ def tile_fusedqkvfp8linear_kernel(
         nc.sync.dma_start(out=rows[0:6, :], in_=w_scale.rearrange("o (r c) -> (o r) c", c=NB))
         nc.sync.dma_start(out=rows[6:12, :], in_=bias.rearrange("(r c) -> r c", c=NB))
         make_identity(nc, ident_b[:])
-
-        def load_scales(jp):
-            nc.vector.memset(w_planes[jp][:].bitcast(I32), 0)
-            for r in range(4):
-                nc.gpsimd.dma_start(
-                    out=w_planes[jp][r:P:32, :, :].bitcast(F32),
-                    in_=scales_f32[r][:, :, N_OUT // 4 * jp : N_OUT // 4 * (jp + 1)],
-                )
-
-        load_scales(0)
         make_identity(nc, ident_f[:])
-        load_scales(1)
-        load_scales(2)
 
         def load_x(mt):
             nc.sync.dma_start(out=x_sb[mt][:], in_=x[P * mt : P * (mt + 1), :])
 
         def load_weight(c):
             j0, j1 = CHUNKS[c]
+            nc.vector.memset(w_planes[c][:].bitcast(I32), 0)
+            for r in range(4):
+                nc.sync.dma_start(
+                    out=w_planes[c][r:P:32, :, :].bitcast(I32),
+                    in_=scales_i32[r][:, :, NB // 4 * j0 : NB // 4 * j1],
+                )
             nc.sync.dma_start(out=w_sb[c][:].bitcast(I32), in_=words_i32[:, :, NB // 2 * j0 : NB // 2 * j1])
 
         load_x(0)
@@ -87,6 +83,9 @@ def tile_fusedqkvfp8linear_kernel(
         load_x(3)
         load_weight(2)
         load_weight(3)
+
+        res_tiles = {}
+        finished = []
 
         def spread_rows(r0):
             bank = ps_small.tile([P, 2 * NB], BF16, tag="small")
@@ -134,19 +133,22 @@ def tile_fusedqkvfp8linear_kernel(
                     lhsT=x_codes[:, mt, g, :].bitcast(FP8X4),
                     lhsT_scale=x_planes[:, mt, g, :],
                     rhs=w_sb[c][:, g, 2 * NB * i : 2 * NB * (i + 1)].bitcast(FP4X4),
-                    rhs_scale=w_planes[j // 2][:, g, NB * (j % 2) : NB * (j % 2 + 1)],
+                    rhs_scale=w_planes[c][:, g, NB * i : NB * (i + 1)],
                     start=(g == 0),
                     stop=(g == G - 1),
                 )
-            res = results.tile([P, NB], F32, tag="res")
-            nc.vector.tensor_tensor(out=res[:], in0=acc[:], in1=spread[:, NB * j : NB * (j + 1)], op=MULT)
-            return res
+            if (mt, j // 2) not in res_tiles:
+                res_tiles[(mt, j // 2)] = results.tile([P, N_OUT], F32, tag="res", name="res")
+            half = res_tiles[(mt, j // 2)][:, NB * (j % 2) : NB * (j % 2 + 1)]
+            nc.vector.tensor_tensor(out=half, in0=acc[:], in1=spread[:, NB * j : NB * (j + 1)], op=MULT)
 
-        def finish(mt, j, res):
-            nc.vector.tensor_tensor(out=res[:], in0=res[:], in1=spread[:, N + NB * j : N + NB * (j + 1)], op=ADD)
-            nc.sync.dma_start(
-                out=outs[j // 2][P * mt : P * (mt + 1), NB * (j % 2) : NB * (j % 2 + 1)], in_=res[:]
-            )
+        def finish(mt, j):
+            res = res_tiles[(mt, j // 2)]
+            half = res[:, NB * (j % 2) : NB * (j % 2 + 1)]
+            nc.vector.tensor_tensor(out=half, in0=half, in1=spread[:, N + NB * j : N + NB * (j + 1)], op=ADD)
+            finished.append((mt, j // 2))
+            if finished.count((mt, j // 2)) == 2:
+                nc.sync.dma_start(out=outs[j // 2][P * mt : P * (mt + 1), :], in_=res[:])
 
         jobs = [(0, 0), (1, 0), (0, 1), (1, 1), (2, 0), (2, 1), (3, 0), (3, 1)]
         jobs.extend((mt, j) for jp in (1, 2) for mt in range(MT) for j in (2 * jp, 2 * jp + 1))
@@ -159,13 +161,16 @@ def tile_fusedqkvfp8linear_kernel(
         quantise_x(0, grouped)
         waiting = None
         for n, (mt, j) in enumerate(jobs):
+            if n == len(jobs) - 1:
+                finish(*waiting)
+                waiting = None
             if n == 1:
                 spread_rows(4)
                 spread_rows(10)
             if n in (1, 4, 6):
                 quantise_x(mt, transpose_x(mt))
-            res = multiply(mt, j)
+            multiply(mt, j)
             if waiting is not None:
                 finish(*waiting)
-            waiting = (mt, j, res)
+            waiting = (mt, j)
         finish(*waiting)

from contextlib import ExitStack

import concourse.mybir as mybir
from concourse.masks import make_identity

F32 = mybir.dt.float32
BF16 = mybir.dt.bfloat16
I32 = mybir.dt.int32
U32 = mybir.dt.uint32
U8 = mybir.dt.uint8
FP8X4 = mybir.dt.float8_e4m3fn_x4
FP4X4 = mybir.dt.float4_e2m1fn_x4
MULT = mybir.AluOpType.mult
ADD = mybir.AluOpType.add

P = 128
M, K, N = 512, 3072, 3072
K_PASS = 512
G = K // K_PASS
MT = M // P
NB = 512
N_OUT = 1024
FLOPS = 2 * M * K * N


CHUNKS = ((0, 1), (1, 2), (2, 4), (4, 6))


def tile_fusedqkvfp8linear_kernel(
    tc, x, weight_fp8_t_words, weight_fp8_t_scales, w_scale, bias, out_0, out_1, out_2
):
    nc = tc.nc
    outs = (out_0, out_1, out_2)
    words_i32 = weight_fp8_t_words.bitcast(I32).rearrange("g p b -> p g b")
    scales_i32 = weight_fp8_t_scales.bitcast(I32).rearrange("g (q r) n -> r q g n", r=4)

    with ExitStack() as ctx:
        ctx.enter_context(tc.manual_schedule())
        keep = ctx.enter_context(tc.tile_pool(name="keep", bufs=1))
        stage = ctx.enter_context(tc.tile_pool(name="stage", bufs=4))
        results = ctx.enter_context(tc.tile_pool(name="results", bufs=8))
        ps_small = ctx.enter_context(tc.psum_pool(name="ps_small", bufs=3))
        ps_acc = ctx.enter_context(tc.psum_pool(name="ps_acc", bufs=5))

        x_sb = [keep.tile([P, K], BF16, name="x_sb%d" % mt) for mt in range(MT)]
        w_sb = [
            keep.tile([P, G, 2 * NB * (j1 - j0)], U8, align_bytes=64, name="w_sb%d" % j0) for j0, j1 in CHUNKS
        ]
        w_planes = [
            keep.tile([P, G, NB * (j1 - j0)], U8, align_bytes=64, name="w_planes%d" % j0) for j0, j1 in CHUNKS
        ]
        x_codes = keep.tile([P, MT, G, P], U32, align_bytes=64)
        x_planes = keep.tile([P, MT, G, P], U8, align_bytes=64)
        ident_b = keep.tile([P, P], BF16)
        ident_f = keep.tile([P, P], F32)
        rows = keep.tile([P, NB], BF16)
        spread = keep.tile([P, 2 * N], BF16)

        nc.gpsimd.memset(rows[:], 0.0)
        nc.sync.dma_start(out=rows[0:6, :], in_=w_scale.rearrange("o (r c) -> (o r) c", c=NB))
        nc.sync.dma_start(out=rows[6:12, :], in_=bias.rearrange("(r c) -> r c", c=NB))
        make_identity(nc, ident_b[:])
        make_identity(nc, ident_f[:])

        def load_x(mt):
            nc.sync.dma_start(out=x_sb[mt][:], in_=x[P * mt : P * (mt + 1), :])

        def load_weight(c):
            j0, j1 = CHUNKS[c]
            nc.vector.memset(w_planes[c][:].bitcast(I32), 0)
            for r in range(4):
                nc.sync.dma_start(
                    out=w_planes[c][r:P:32, :, :].bitcast(I32),
                    in_=scales_i32[r][:, :, NB // 4 * j0 : NB // 4 * j1],
                )
            nc.sync.dma_start(out=w_sb[c][:].bitcast(I32), in_=words_i32[:, :, NB // 2 * j0 : NB // 2 * j1])

        load_x(0)
        load_weight(0)
        load_x(1)
        load_weight(1)
        load_x(2)
        load_x(3)
        load_weight(2)
        load_weight(3)

        res_tiles = {}
        finished = []

        def spread_rows(r0):
            bank = ps_small.tile([P, 2 * NB], BF16, tag="small")
            for i in range(2):
                nc.tensor.matmul(
                    out=bank[:, NB * i : NB * (i + 1)],
                    lhsT=ident_b[:, r0 + i : r0 + i + 1].to_broadcast([P, P]),
                    rhs=rows[:],
                    start=True,
                    stop=True,
                )
            nc.scalar.copy(out=spread[:, NB * r0 : NB * (r0 + 2)], in_=bank[:])

        def transpose_x(mt):
            x_words = x_sb[mt][:].bitcast(F32)
            grouped = []
            for h in range(G // 2):
                bank = ps_small.tile([P, 2, 2, P], F32, tag="small")
                for gg in range(2):
                    g = 2 * h + gg
                    for u in range(2):
                        nc.tensor.transpose(
                            bank[:, gg, u, :], x_words[:, 256 * g + u : 256 * (g + 1) : 2], ident_f[:]
                        )
                gr = stage.tile([P, 2, P, 4], BF16, align_bytes=64, tag="grouped")
                nc.scalar.copy(out=gr[:].bitcast(F32), in_=bank[:].rearrange("p g u m -> p g m u"))
                grouped.append(gr)
            return grouped

        def quantise_x(mt, grouped):
            for h in range(G // 2):
                nc.vector.quantize_mx(
                    out=x_codes[:, mt, 2 * h : 2 * h + 2, :].rearrange("p g m -> p (g m)").bitcast(FP8X4),
                    scales=x_planes[:, mt, 2 * h : 2 * h + 2, :].rearrange("p g m -> p (g m)"),
                    in_=grouped[h][:].rearrange("p g m t -> p (g m t)"),
                )

        def multiply(mt, j):
            c = [i for i in range(len(CHUNKS)) if CHUNKS[i][0] <= j < CHUNKS[i][1]][0]
            i = j - CHUNKS[c][0]
            acc = ps_acc.tile([P, NB], F32, tag="acc")
            for g in range(G):
                nc.tensor.matmul_mx(
                    out=acc[:],
                    lhsT=x_codes[:, mt, g, :].bitcast(FP8X4),
                    lhsT_scale=x_planes[:, mt, g, :],
                    rhs=w_sb[c][:, g, 2 * NB * i : 2 * NB * (i + 1)].bitcast(FP4X4),
                    rhs_scale=w_planes[c][:, g, NB * i : NB * (i + 1)],
                    start=(g == 0),
                    stop=(g == G - 1),
                )
            if (mt, j // 2) not in res_tiles:
                res_tiles[(mt, j // 2)] = results.tile([P, N_OUT], F32, tag="res", name="res")
            half = res_tiles[(mt, j // 2)][:, NB * (j % 2) : NB * (j % 2 + 1)]
            nc.vector.tensor_tensor(out=half, in0=acc[:], in1=spread[:, NB * j : NB * (j + 1)], op=MULT)

        def finish(mt, j):
            res = res_tiles[(mt, j // 2)]
            half = res[:, NB * (j % 2) : NB * (j % 2 + 1)]
            nc.vector.tensor_tensor(out=half, in0=half, in1=spread[:, N + NB * j : N + NB * (j + 1)], op=ADD)
            finished.append((mt, j // 2))
            if finished.count((mt, j // 2)) == 2:
                nc.sync.dma_start(out=outs[j // 2][P * mt : P * (mt + 1), :], in_=res[:])

        jobs = [(0, 0), (1, 0), (0, 1), (1, 1), (2, 0), (2, 1), (3, 0), (3, 1)]
        jobs.extend((mt, j) for jp in (1, 2) for mt in range(MT) for j in (2 * jp, 2 * jp + 1))

        spread_rows(0)
        spread_rows(6)
        grouped = transpose_x(0)
        spread_rows(2)
        spread_rows(8)
        quantise_x(0, grouped)
        waiting = None
        for n, (mt, j) in enumerate(jobs):
            if n == len(jobs) - 1:
                finish(*waiting)
                waiting = None
            if n == 1:
                spread_rows(4)
                spread_rows(10)
            if n in (1, 4, 6):
                quantise_x(mt, transpose_x(mt))
            multiply(mt, j)
            if waiting is not None:
                finish(*waiting)
            waiting = (mt, j)
        finish(*waiting)
